import numpy as np
import ml_dtypes


def mxq(x, axis, fmt="e4m3"):
    dtype, down = {"e4m3": (ml_dtypes.float8_e4m3fn, 7), "e5m2": (ml_dtypes.float8_e5m2, 14)}[fmt]
    v = np.moveaxis(np.asarray(x, np.float32).astype(ml_dtypes.bfloat16).astype(np.float64), axis, -1)
    blocks = v.reshape(v.shape[:-1] + (-1, 32))
    amax = np.abs(blocks).max(-1, keepdims=True)
    byte = np.maximum(np.where(amax > 0, np.frexp(amax)[1] - 1 + 127, 0) - down, 1)
    scale = np.exp2(byte - 127.0)
    codes = (blocks / scale).astype(np.float32).astype(dtype).astype(np.float64)
    return np.moveaxis((codes * scale).reshape(v.shape), -1, axis)


WIDE = False


def mx_kscale(k):
    if not WIDE:
        return np.ones(k)
    levels = np.array([10, -10, 5, -5, 0])
    a = np.random.permutation(np.resize(levels, k // 512 * 4)).reshape(k // 512, 4)
    idx = np.arange(k)
    return np.exp2(a[idx // 512, idx % 128 // 32])


BF16 = ml_dtypes.bfloat16


def bf(x):
    return np.asarray(x, np.float32).astype(BF16)


def f64(x):
    return np.asarray(x).astype(np.float64)


B, S, D, H, QL, KVL, RD, ND, VD = 2, 2048, 1024, 4, 1536, 512, 128, 64, 64
ROPE_THETA, ROPE_RATIO = 10000.0, 1.0


def rope_tables(seq_len):
    half = RD // 2
    inv_freq = ROPE_RATIO / (ROPE_THETA ** (np.arange(half) * 2.0 / RD))
    freqs = np.arange(seq_len)[:, None] * inv_freq[None, :]
    return np.cos(freqs), np.sin(freqs)


def apply_rope(x, cos, sin):
    x_even = x[..., 0::2]
    x_odd = x[..., 1::2]
    r_even = x_even * cos - x_odd * sin
    r_odd = x_odd * cos + x_even * sin
    return np.stack([r_even, r_odd], axis=-1).reshape(x.shape)


def setup_inputs():
    s, t = mx_kscale(D), mx_kscale(KVL)
    tc = np.concatenate([t, np.ones(RD)])
    return {"hidden_states": bf(np.random.standard_normal((B, S, D)) * s),
            "Wkva": bf(np.random.standard_normal((D, KVL + RD)) / np.sqrt(D) / s[:, None] * tc),
            "Wkvb": bf(np.random.standard_normal((KVL, H * (ND + VD))) / np.sqrt(KVL) / t[:, None])}


def reference(hidden_states, Wkva, Wkvb):
    kv_comp = mxq(f64(hidden_states), 2, "e4m3") @ mxq(f64(Wkva), 0, "e4m3")
    c_kv, k_pe = kv_comp[..., :KVL], kv_comp[..., KVL:]
    cos, sin = rope_tables(S)
    k_pe = apply_rope(k_pe, cos, sin)
    kv = (mxq(c_kv, 2, "e4m3") @ mxq(f64(Wkvb), 0, "e4m3")).reshape(B, S, H, ND + VD)
    kv = kv.transpose(0, 2, 1, 3)
    k_nope, v = kv[..., :ND], kv[..., ND:]
    k_pe_b = np.broadcast_to(k_pe[:, None], (B, H, S, RD))
    k_full = np.concatenate([k_nope, k_pe_b], axis=-1)
    return k_full, v

@@ -1,0 +1,367 @@
+import math
+from contextlib import ExitStack
+
+import concourse.mybir as mybir
+from concourse.masks import make_identity
+
+F32 = mybir.dt.float32
+BF16 = mybir.dt.bfloat16
+I32 = mybir.dt.int32
+U32 = mybir.dt.uint32
+U8 = mybir.dt.uint8
+FP8X4 = mybir.dt.float8_e4m3fn_x4
+ALU = mybir.AluOpType
+ACT = mybir.ActivationFunctionType
+
+P = 128
+PACK = 4
+
+BATCH, SEQ, D_MODEL = 2, 2048, 1024
+HEADS, LATENT, ROPE_DIM, NOPE_DIM, V_DIM = 4, 512, 128, 64, 64
+ROPE_THETA = 10000.0
+ROPE_PAIRS = ROPE_DIM // 2
+
+PASSES = D_MODEL // (P * PACK)
+LATENT_TILES = LATENT // P
+
+SLOTS = 4
+GROUP = P * SLOTS
+GROUPS = BATCH * SEQ // GROUP
+GROUPS_PER_BATCH = SEQ // GROUP
+TABLE_SLOTS = GROUPS_PER_BATCH * SLOTS
+
+STEP_SLOTS = 2
+STEP_TOKENS = STEP_SLOTS * P
+STEPS_PER_GROUP = SLOTS // STEP_SLOTS
+STEPS = GROUPS * STEPS_PER_GROUP
+
+ROUND_MAGIC = 12582912.0
+
+FLOPS = 2 * BATCH * SEQ * (D_MODEL * (LATENT + ROPE_DIM) + LATENT * HEADS * (NOPE_DIM + V_DIM))
+
+
+def build_rope_tables(nc, pool, cos_tab, sin_tab):
+    position_int = pool.tile([P, TABLE_SLOTS], I32)
+    nc.gpsimd.iota(
+        position_int[:], pattern=[[GROUP, GROUPS_PER_BATCH], [1, SLOTS]], base=0, channel_multiplier=SLOTS
+    )
+    position = pool.tile([P, TABLE_SLOTS], F32)
+    nc.vector.tensor_copy(out=position[:], in_=position_int[:])
+
+    ones = pool.tile([P, 8], F32)
+    nc.vector.memset(ones[:], 1.0)
+    coarse = pool.tile([P, 8], F32)
+    fine = pool.tile([P, 8], F32)
+    for a in range(8):
+        nc.vector.tensor_scalar(
+            out=coarse[:, a : a + 1], in0=ones[:, a : a + 1],
+            scalar1=ROPE_THETA ** (-2.0 * 8 * a / ROPE_DIM) / (2.0 * math.pi), scalar2=None, op0=ALU.mult,
+        )
+        nc.vector.tensor_scalar(
+            out=fine[:, a : a + 1], in0=ones[:, a : a + 1],
+            scalar1=ROPE_THETA ** (-2.0 * a / ROPE_DIM), scalar2=None, op0=ALU.mult,
+        )
+    half_pi = pool.tile([P, 1], F32)
+    nc.vector.tensor_scalar(out=half_pi[:], in0=ones[:, 0:1], scalar1=math.pi / 2.0, scalar2=None, op0=ALU.mult)
+    sign = pool.tile([P, 2], F32)
+    nc.vector.memset(sign[:, 0:1], -1.0)
+    nc.vector.memset(sign[:, 1:2], 1.0)
+
+    turns_per_position = pool.tile([P, 8, 8], F32)
+    nc.vector.tensor_tensor(
+        out=turns_per_position[:],
+        in0=coarse[:].unsqueeze(2).to_broadcast([P, 8, 8]),
+        in1=fine[:].unsqueeze(1).to_broadcast([P, 8, 8]),
+        op=ALU.mult,
+    )
+    table_shape = [P, TABLE_SLOTS, ROPE_PAIRS]
+    turns = pool.tile(table_shape, F32)
+    nc.vector.tensor_tensor(
+        out=turns[:],
+        in0=position[:].unsqueeze(2).to_broadcast(table_shape),
+        in1=turns_per_position[:].rearrange("p a b -> p (a b)").unsqueeze(1).to_broadcast(table_shape),
+        op=ALU.mult,
+    )
+    whole_turns = pool.tile(table_shape, F32)
+    nc.vector.tensor_scalar(
+        out=whole_turns[:], in0=turns[:], scalar1=ROUND_MAGIC, scalar2=ROUND_MAGIC, op0=ALU.add, op1=ALU.subtract
+    )
+    fraction = pool.tile(table_shape, F32)
+    nc.vector.tensor_tensor(out=fraction[:], in0=turns[:], in1=whole_turns[:], op=ALU.subtract)
+
+    signed_fraction = pool.tile([P, TABLE_SLOTS * ROPE_PAIRS, 2], F32)
+    nc.vector.tensor_tensor(
+        out=signed_fraction[:],
+        in0=fraction[:].rearrange("p n i -> p (n i)").unsqueeze(2).to_broadcast([P, TABLE_SLOTS * ROPE_PAIRS, 2]),
+        in1=sign[:].unsqueeze(1).to_broadcast([P, TABLE_SLOTS * ROPE_PAIRS, 2]),
+        op=ALU.mult,
+    )
+    nc.scalar.activation(
+        out=sin_tab[:].rearrange("p n d -> p (n d)"),
+        in_=signed_fraction[:].rearrange("p m e -> p (m e)"),
+        func=ACT.Sin,
+        scale=2.0 * math.pi,
+    )
+
+    magnitude = pool.tile(table_shape, F32)
+    nc.vector.scalar_tensor_tensor(
+        out=magnitude[:].rearrange("p n i -> p (n i)"),
+        in0=fraction[:].rearrange("p n i -> p (n i)"),
+        scalar=-1.0,
+        in1=fraction[:].rearrange("p n i -> p (n i)"),
+        op0=ALU.mult,
+        op1=ALU.max,
+    )
+    nc.scalar.activation(
+        out=cos_tab[:].rearrange("p n i -> p (n i)"),
+        in_=magnitude[:].rearrange("p n i -> p (n i)"),
+        func=ACT.Sin,
+        bias=half_pi[:, 0:1],
+        scale=-2.0 * math.pi,
+    )
+
+
+def tile_mlaattention_pb_t_kernel(tc, hidden_states, Wkva, Wkvb, out_0, out_1):
+    nc = tc.nc
+    with ExitStack() as ctx:
+        const = ctx.enter_context(tc.tile_pool(name="const", bufs=1))
+        x_pool = ctx.enter_context(tc.tile_pool(name="x_pool", bufs=GROUPS))
+        stage = ctx.enter_context(tc.tile_pool(name="stage", bufs=2))
+        out_pool = ctx.enter_context(tc.tile_pool(name="out_pool", bufs=3))
+        psum_xt = ctx.enter_context(tc.psum_pool(name="psum_xt", bufs=2))
+        psum_c = ctx.enter_context(tc.psum_pool(name="psum_c", bufs=2))
+        psum_rope = ctx.enter_context(tc.psum_pool(name="psum_rope", bufs=1))
+        psum_kv = ctx.enter_context(tc.psum_pool(name="psum_kv", bufs=3))
+
+        x_groups = hidden_states.flatten_outer_dims().rearrange("(g p t) d -> g p (t d)", p=P, t=SLOTS)
+        k_groups = [
+            out_0[g // GROUPS_PER_BATCH, :, (g % GROUPS_PER_BATCH) * GROUP : (g % GROUPS_PER_BATCH + 1) * GROUP, :]
+            .rearrange("h (p t) d -> p h (t d)", t=SLOTS)
+            for g in range(GROUPS)
+        ]
+        v_groups = [
+            out_1[g // GROUPS_PER_BATCH, :, (g % GROUPS_PER_BATCH) * GROUP : (g % GROUPS_PER_BATCH + 1) * GROUP, :]
+            .rearrange("h (p t) d -> p h (t d)", t=SLOTS)
+            for g in range(GROUPS)
+        ]
+
+        x_tiles = []
+        wa_raw = const.tile([P, PASSES, PACK, LATENT + ROPE_DIM], BF16)
+        wb_raw = const.tile([P, PACK, LATENT], BF16)
+        for g in range(GROUPS):
+            x_sb = x_pool.tile([P, SLOTS, D_MODEL], BF16)
+            nc.sync.dma_start(out=x_sb[:].rearrange("p t d -> p (t d)"), in_=x_groups[g])
+            x_tiles.append(x_sb)
+            if g == 0:
+                nc.sync.dma_start(
+                    out=wa_raw[:].rearrange("q c (u e) n -> q (c u) (e n)", e=2),
+                    in_=Wkva.rearrange("(c u q e) n -> q (c u) (e n)", c=PASSES, u=2, e=2),
+                )
+                nc.sync.dma_start(out=wb_raw[:], in_=Wkvb.rearrange("(j q) n -> q j n", q=P))
+
+        ident = const.tile([P, P], F32)
+        make_identity(nc, ident[:])
+
+        cos_tab = const.tile([P, TABLE_SLOTS, ROPE_PAIRS], F32)
+        sin_tab = const.tile([P, TABLE_SLOTS, ROPE_DIM], F32)
+        build_rope_tables(nc, const, cos_tab, sin_tab)
+
+        wl_grouped = const.tile([P, PASSES, LATENT, PACK], BF16, align_bytes=64)
+        wr_grouped = const.tile([P, PASSES, ROPE_DIM, PACK], BF16, align_bytes=64)
+        wb_grouped = const.tile([P, 2, HEADS, NOPE_DIM, PACK], BF16, align_bytes=64)
+        wl_codes = const.tile([P, PASSES, LATENT], U32, align_bytes=64)
+        wl_scales = const.tile([P, PASSES, LATENT], U8, align_bytes=64)
+        wr_codes = const.tile([P, PASSES, ROPE_DIM], U32, align_bytes=64)
+        wr_scales = const.tile([P, PASSES, ROPE_DIM], U8, align_bytes=64)
+        wb_codes = const.tile([P, LATENT], U32, align_bytes=64)
+        wb_scales = const.tile([P, LATENT], U8, align_bytes=64)
+
+        nc.vector.tensor_copy(out=wl_grouped[:, 0], in_=wa_raw[:, 0, :, 0:LATENT].rearrange("p j n -> p n j"))
+        nc.scalar.copy(out=wl_grouped[:, 1], in_=wa_raw[:, 1, :, 0:LATENT].rearrange("p j n -> p n j"))
+        nc.vector.tensor_copy(out=wr_grouped[:], in_=wa_raw[:, :, :, LATENT:].rearrange("p c j n -> p c n j"))
+        wb_parts = wb_raw[:].rearrange("p j (h two d) -> p two h d j", two=2, d=NOPE_DIM)
+        for part in range(2):
+            nc.vector.tensor_copy(out=wb_grouped[:, part], in_=wb_parts[:, part])
+        nc.vector.quantize_mx(
+            out=wl_codes[:].rearrange("p c n -> p (c n)").bitcast(FP8X4),
+            scales=wl_scales[:].rearrange("p c n -> p (c n)"),
+            in_=wl_grouped[:].rearrange("p c n j -> p (c n j)"),
+        )
+        nc.vector.quantize_mx(
+            out=wr_codes[:].rearrange("p c n -> p (c n)").bitcast(FP8X4),
+            scales=wr_scales[:].rearrange("p c n -> p (c n)"),
+            in_=wr_grouped[:].rearrange("p c n j -> p (c n j)"),
+        )
+        nc.vector.quantize_mx(
+            out=wb_codes[:].bitcast(FP8X4),
+            scales=wb_scales[:],
+            in_=wb_grouped[:].rearrange("p two h d j -> p (two h d j)"),
+        )
+
+        live = {}
+
+        def slots_of(step):
+            first = (step % STEPS_PER_GROUP) * STEP_SLOTS
+            return step // STEPS_PER_GROUP, first
+
+        def transpose_x(step):
+            group, first = slots_of(step)
+            x_grouped = stage.tile([P, PASSES, STEP_TOKENS, 2], F32, align_bytes=64)
+            for s in range(STEP_SLOTS):
+                x_words = x_tiles[group][:, first + s, :].bitcast(F32)
+                xt = psum_xt.tile([P, PASSES * 2, P], F32)
+                for block in range(PASSES * 2):
+                    nc.tensor.transpose(xt[:, block, :], x_words[:, block * P : (block + 1) * P], ident[:])
+                nc.scalar.copy(
+                    out=x_grouped[:, :, s * P : (s + 1) * P, :],
+                    in_=xt[:].rearrange("q (c u) r -> q c r u", u=2),
+                )
+            live["x_grouped", step] = x_grouped
+
+        def quantise_x(step):
+            x_codes = stage.tile([P, PASSES, STEP_TOKENS], U32, align_bytes=64)
+            x_scales = stage.tile([P, PASSES, STEP_TOKENS], U8, align_bytes=64)
+            nc.vector.quantize_mx(
+                out=x_codes[:].rearrange("p c r -> p (c r)").bitcast(FP8X4),
+                scales=x_scales[:].rearrange("p c r -> p (c r)"),
+                in_=live["x_grouped", step][:].rearrange("p c r u -> p (c r u)").bitcast(BF16),
+            )
+            live["x_codes", step] = (x_codes, x_scales)
+
+        def project(step):
+            x_codes, x_scales = live["x_codes", step]
+            c_grouped = stage.tile([P, STEP_TOKENS, PACK], BF16, align_bytes=64)
+            for s in range(STEP_SLOTS):
+                tokens = slice(s * P, (s + 1) * P)
+                c_ps = psum_c.tile([P, LATENT_TILES, P], F32)
+                for j in range(LATENT_TILES):
+                    for c in range(PASSES):
+                        nc.tensor.matmul_mx(
+                            out=c_ps[:, j, :],
+                            lhsT=wl_codes[:, c, j * P : (j + 1) * P].bitcast(FP8X4),
+                            lhsT_scale=wl_scales[:, c, j * P : (j + 1) * P],
+                            rhs=x_codes[:, c, tokens].bitcast(FP8X4),
+                            rhs_scale=x_scales[:, c, tokens],
+                            start=(c == 0),
+                            stop=(c == PASSES - 1),
+                        )
+                nc.scalar.copy(out=c_grouped[:, tokens, :], in_=c_ps[:].rearrange("q j r -> q r j"))
+            rope_ps = psum_rope.tile([P, STEP_SLOTS, ROPE_DIM], F32)
+            for s in range(STEP_SLOTS):
+                tokens = slice(s * P, (s + 1) * P)
+                for c in range(PASSES):
+                    nc.tensor.matmul_mx(
+                        out=rope_ps[:, s, :],
+                        lhsT=x_codes[:, c, tokens].bitcast(FP8X4),
+                        lhsT_scale=x_scales[:, c, tokens],
+                        rhs=wr_codes[:, c, :].bitcast(FP8X4),
+                        rhs_scale=wr_scales[:, c, :],
+                        start=(c == 0),
+                        stop=(c == PASSES - 1),
+                    )
+            live["c_grouped", step] = c_grouped
+            live["rope_ps", step] = rope_ps
+
+        def quantise_c(step):
+            c_codes = stage.tile([P, STEP_TOKENS], U32, align_bytes=64)
+            c_scales = stage.tile([P, STEP_TOKENS], U8, align_bytes=64)
+            nc.vector.quantize_mx(
+                out=c_codes[:].bitcast(FP8X4),
+                scales=c_scales[:],
+                in_=live["c_grouped", step][:].rearrange("p r j -> p (r j)"),
+            )
+            live["c_codes", step] = (c_codes, c_scales)
+
+        def rotate(step):
+            group, first = slots_of(step)
+            if first == 0:
+                k_out = out_pool.tile([P, HEADS, SLOTS, NOPE_DIM + ROPE_DIM], F32)
+                v_out = out_pool.tile([P, HEADS, SLOTS, V_DIM], F32)
+                live["out", group] = (k_out, v_out)
+            k_out, v_out = live["out", group]
+            table = (group % GROUPS_PER_BATCH) * SLOTS + first
+            pair_shape = [P, STEP_SLOTS, ROPE_PAIRS, 2]
+            rope_pairs = live["rope_ps", step][:].rearrange("p s (i e) -> p s i e", e=2)
+            by_cos = stage.tile(pair_shape, F32)
+            by_sin = stage.tile(pair_shape, F32)
+            nc.vector.tensor_tensor(
+                out=by_cos[:],
+                in0=rope_pairs,
+                in1=cos_tab[:, table : table + STEP_SLOTS, :].unsqueeze(3).to_broadcast(pair_shape),
+                op=ALU.mult,
+            )
+            nc.vector.tensor_tensor(
+                out=by_sin[:],
+                in0=rope_pairs[:, :, :, ::-1],
+                in1=sin_tab[:, table : table + STEP_SLOTS, :].rearrange("p s (i e) -> p s i e", e=2),
+                op=ALU.mult,
+            )
+            nc.vector.tensor_tensor(
+                out=k_out[:, 0, first : first + STEP_SLOTS, NOPE_DIM:],
+                in0=by_cos[:].rearrange("p s i e -> p s (i e)"),
+                in1=by_sin[:].rearrange("p s i e -> p s (i e)"),
+                op=ALU.add,
+            )
+
+        def repeat_for_heads(step):
+            group, first = slots_of(step)
+            k_out, v_out = live["out", group]
+            nc.scalar.copy(
+                out=k_out[:, 1:HEADS, first : first + STEP_SLOTS, NOPE_DIM:],
+                in_=k_out[:, 0:1, first : first + STEP_SLOTS, NOPE_DIM:].to_broadcast(
+                    [P, HEADS - 1, STEP_SLOTS, ROPE_DIM]
+                ),
+            )
+
+        def expand(step):
+            c_codes, c_scales = live["c_codes", step]
+            nope_ps = psum_kv.tile([P, STEP_SLOTS, HEADS * NOPE_DIM], F32, tag="kv")
+            v_ps = psum_kv.tile([P, STEP_SLOTS, HEADS * V_DIM], F32, tag="kv")
+            half = HEADS * NOPE_DIM
+            for s in range(STEP_SLOTS):
+                tokens = slice(s * P, (s + 1) * P)
+                for part, bank in enumerate((nope_ps, v_ps)):
+                    nc.tensor.matmul_mx(
+                        out=bank[:, s, :],
+                        lhsT=c_codes[:, tokens].bitcast(FP8X4),
+                        lhsT_scale=c_scales[:, tokens],
+                        rhs=wb_codes[:, part * half : (part + 1) * half].bitcast(FP8X4),
+                        rhs_scale=wb_scales[:, part * half : (part + 1) * half],
+                        start=True,
+                        stop=True,
+                    )
+            live["kv_ps", step] = (nope_ps, v_ps)
+
+        def finish(step):
+            group, first = slots_of(step)
+            nope_ps, v_ps = live["kv_ps", step]
+            k_out, v_out = live["out", group]
+            nc.vector.tensor_copy(
+                out=k_out[:, :, first : first + STEP_SLOTS, 0:NOPE_DIM].rearrange("p h s d -> p s h d"),
+                in_=nope_ps[:].rearrange("p s (h d) -> p s h d", h=HEADS),
+            )
+            nc.vector.tensor_copy(
+                out=v_out[:, :, first : first + STEP_SLOTS, :].rearrange("p h s d -> p s h d"),
+                in_=v_ps[:].rearrange("p s (h d) -> p s h d", h=HEADS),
+            )
+            if first + STEP_SLOTS == SLOTS:
+                nc.sync.dma_start(out=k_groups[group], in_=k_out[:].rearrange("p h t d -> p h (t d)"))
+                nc.sync.dma_start(out=v_groups[group], in_=v_out[:].rearrange("p h t d -> p h (t d)"))
+
+        for i in range(STEPS + 3):
+            if 0 <= i - 2 < STEPS:
+                rotate(i - 2)
+            if i < STEPS:
+                transpose_x(i)
+            if 0 <= i - 2 < STEPS:
+                repeat_for_heads(i - 2)
+            if 0 <= i - 3 < STEPS:
+                finish(i - 3)
+            if 0 <= i - 1 < STEPS:
+                project(i - 1)
+            if i < STEPS:
+                quantise_x(i)
+            if 0 <= i - 2 < STEPS:
+                expand(i - 2)
+            if 0 <= i - 1 < STEPS:
+                quantise_c(i - 1)

@@ -28,7 +28,6 @@ SLOTS = 4
 GROUP = P * SLOTS
 GROUPS = BATCH * SEQ // GROUP
 GROUPS_PER_BATCH = SEQ // GROUP
-TABLE_SLOTS = GROUPS_PER_BATCH * SLOTS
 
 STEP_SLOTS = 2
 STEP_TOKENS = STEP_SLOTS * P
@@ -36,89 +35,9 @@ STEPS_PER_GROUP = SLOTS // STEP_SLOTS
 STEPS = GROUPS * STEPS_PER_GROUP
 
 ROUND_MAGIC = 12582912.0
+RUN = 4
 
 FLOPS = 2 * BATCH * SEQ * (D_MODEL * (LATENT + ROPE_DIM) + LATENT * HEADS * (NOPE_DIM + V_DIM))
-
-
-def build_rope_tables(nc, pool, cos_tab, sin_tab):
-    position_int = pool.tile([P, TABLE_SLOTS], I32)
-    nc.gpsimd.iota(
-        position_int[:], pattern=[[GROUP, GROUPS_PER_BATCH], [1, SLOTS]], base=0, channel_multiplier=SLOTS
-    )
-    position = pool.tile([P, TABLE_SLOTS], F32)
-    nc.vector.tensor_copy(out=position[:], in_=position_int[:])
-
-    ones = pool.tile([P, 8], F32)
-    nc.vector.memset(ones[:], 1.0)
-    coarse = pool.tile([P, 8], F32)
-    fine = pool.tile([P, 8], F32)
-    for a in range(8):
-        nc.vector.tensor_scalar(
-            out=coarse[:, a : a + 1], in0=ones[:, a : a + 1],
-            scalar1=ROPE_THETA ** (-2.0 * 8 * a / ROPE_DIM) / (2.0 * math.pi), scalar2=None, op0=ALU.mult,
-        )
-        nc.vector.tensor_scalar(
-            out=fine[:, a : a + 1], in0=ones[:, a : a + 1],
-            scalar1=ROPE_THETA ** (-2.0 * a / ROPE_DIM), scalar2=None, op0=ALU.mult,
-        )
-    half_pi = pool.tile([P, 1], F32)
-    nc.vector.tensor_scalar(out=half_pi[:], in0=ones[:, 0:1], scalar1=math.pi / 2.0, scalar2=None, op0=ALU.mult)
-    sign = pool.tile([P, 2], F32)
-    nc.vector.memset(sign[:, 0:1], -1.0)
-    nc.vector.memset(sign[:, 1:2], 1.0)
-
-    turns_per_position = pool.tile([P, 8, 8], F32)
-    nc.vector.tensor_tensor(
-        out=turns_per_position[:],
-        in0=coarse[:].unsqueeze(2).to_broadcast([P, 8, 8]),
-        in1=fine[:].unsqueeze(1).to_broadcast([P, 8, 8]),
-        op=ALU.mult,
-    )
-    table_shape = [P, TABLE_SLOTS, ROPE_PAIRS]
-    turns = pool.tile(table_shape, F32)
-    nc.vector.tensor_tensor(
-        out=turns[:],
-        in0=position[:].unsqueeze(2).to_broadcast(table_shape),
-        in1=turns_per_position[:].rearrange("p a b -> p (a b)").unsqueeze(1).to_broadcast(table_shape),
-        op=ALU.mult,
-    )
-    whole_turns = pool.tile(table_shape, F32)
-    nc.vector.tensor_scalar(
-        out=whole_turns[:], in0=turns[:], scalar1=ROUND_MAGIC, scalar2=ROUND_MAGIC, op0=ALU.add, op1=ALU.subtract
-    )
-    fraction = pool.tile(table_shape, F32)
-    nc.vector.tensor_tensor(out=fraction[:], in0=turns[:], in1=whole_turns[:], op=ALU.subtract)
-
-    signed_fraction = pool.tile([P, TABLE_SLOTS * ROPE_PAIRS, 2], F32)
-    nc.vector.tensor_tensor(
-        out=signed_fraction[:],
-        in0=fraction[:].rearrange("p n i -> p (n i)").unsqueeze(2).to_broadcast([P, TABLE_SLOTS * ROPE_PAIRS, 2]),
-        in1=sign[:].unsqueeze(1).to_broadcast([P, TABLE_SLOTS * ROPE_PAIRS, 2]),
-        op=ALU.mult,
-    )
-    nc.scalar.activation(
-        out=sin_tab[:].rearrange("p n d -> p (n d)"),
-        in_=signed_fraction[:].rearrange("p m e -> p (m e)"),
-        func=ACT.Sin,
-        scale=2.0 * math.pi,
-    )
-
-    magnitude = pool.tile(table_shape, F32)
-    nc.vector.scalar_tensor_tensor(
-        out=magnitude[:].rearrange("p n i -> p (n i)"),
-        in0=fraction[:].rearrange("p n i -> p (n i)"),
-        scalar=-1.0,
-        in1=fraction[:].rearrange("p n i -> p (n i)"),
-        op0=ALU.mult,
-        op1=ALU.max,
-    )
-    nc.scalar.activation(
-        out=cos_tab[:].rearrange("p n i -> p (n i)"),
-        in_=magnitude[:].rearrange("p n i -> p (n i)"),
-        func=ACT.Sin,
-        bias=half_pi[:, 0:1],
-        scale=-2.0 * math.pi,
-    )
 
 
 def tile_mlaattention_pb_t_kernel(tc, hidden_states, Wkva, Wkvb, out_0, out_1):
@@ -126,45 +45,124 @@ def tile_mlaattention_pb_t_kernel(tc, hidden_states, Wkva, Wkvb, out_0, out_1):
     with ExitStack() as ctx:
         const = ctx.enter_context(tc.tile_pool(name="const", bufs=1))
         x_pool = ctx.enter_context(tc.tile_pool(name="x_pool", bufs=GROUPS))
-        stage = ctx.enter_context(tc.tile_pool(name="stage", bufs=2))
+        angle = ctx.enter_context(tc.tile_pool(name="angle", bufs=2))
+        stage = ctx.enter_context(tc.tile_pool(name="stage", bufs=3))
         out_pool = ctx.enter_context(tc.tile_pool(name="out_pool", bufs=3))
         psum_xt = ctx.enter_context(tc.psum_pool(name="psum_xt", bufs=2))
         psum_c = ctx.enter_context(tc.psum_pool(name="psum_c", bufs=2))
         psum_rope = ctx.enter_context(tc.psum_pool(name="psum_rope", bufs=1))
         psum_kv = ctx.enter_context(tc.psum_pool(name="psum_kv", bufs=3))
 
-        x_groups = hidden_states.flatten_outer_dims().rearrange("(g p t) d -> g p (t d)", p=P, t=SLOTS)
-        k_groups = [
-            out_0[g // GROUPS_PER_BATCH, :, (g % GROUPS_PER_BATCH) * GROUP : (g % GROUPS_PER_BATCH + 1) * GROUP, :]
-            .rearrange("h (p t) d -> p h (t d)", t=SLOTS)
-            for g in range(GROUPS)
-        ]
-        v_groups = [
-            out_1[g // GROUPS_PER_BATCH, :, (g % GROUPS_PER_BATCH) * GROUP : (g % GROUPS_PER_BATCH + 1) * GROUP, :]
-            .rearrange("h (p t) d -> p h (t d)", t=SLOTS)
-            for g in range(GROUPS)
-        ]
+        x_groups = hidden_states.flatten_outer_dims().rearrange("(g p t) d -> g p t d", p=P, t=SLOTS)
 
-        x_tiles = []
+        def group_rows(out, group):
+            batch, part = divmod(group, GROUPS_PER_BATCH)
+            rows = out[batch, :, part * GROUP : (part + 1) * GROUP, :]
+            return rows.rearrange("h (p t) d -> p h t d", t=SLOTS)
+
         wa_raw = const.tile([P, PASSES, PACK, LATENT + ROPE_DIM], BF16)
+        wa_rows = Wkva.rearrange("(c u q e) n -> c q u (e n)", c=PASSES, u=2, e=2)
+        for c in range(PASSES):
+            nc.sync.dma_start(out=wa_raw[:, c].rearrange("q (u e) n -> q u (e n)", e=2), in_=wa_rows[c])
         wb_raw = const.tile([P, PACK, LATENT], BF16)
+        x_tiles = []
         for g in range(GROUPS):
             x_sb = x_pool.tile([P, SLOTS, D_MODEL], BF16)
-            nc.sync.dma_start(out=x_sb[:].rearrange("p t d -> p (t d)"), in_=x_groups[g])
             x_tiles.append(x_sb)
             if g == 0:
-                nc.sync.dma_start(
-                    out=wa_raw[:].rearrange("q c (u e) n -> q (c u) (e n)", e=2),
-                    in_=Wkva.rearrange("(c u q e) n -> q (c u) (e n)", c=PASSES, u=2, e=2),
-                )
+                for first in range(0, SLOTS, STEP_SLOTS):
+                    nc.sync.dma_start(
+                        out=x_sb[:, first : first + STEP_SLOTS, :], in_=x_groups[g][:, first : first + STEP_SLOTS, :]
+                    )
                 nc.sync.dma_start(out=wb_raw[:], in_=Wkvb.rearrange("(j q) n -> q j n", q=P))
+            else:
+                nc.sync.dma_start(out=x_sb[:], in_=x_groups[g])
 
         ident = const.tile([P, P], F32)
         make_identity(nc, ident[:])
 
-        cos_tab = const.tile([P, TABLE_SLOTS, ROPE_PAIRS], F32)
-        sin_tab = const.tile([P, TABLE_SLOTS, ROPE_DIM], F32)
-        build_rope_tables(nc, const, cos_tab, sin_tab)
+        cos_tab = const.tile([P, GROUPS_PER_BATCH * SLOTS, ROPE_PAIRS], F32)
+        sin_tab = const.tile([P, GROUPS_PER_BATCH * SLOTS, ROPE_DIM], F32)
+
+        sign = const.tile([P, 2], F32)
+        nc.vector.memset(sign[:, 0:1], -1.0)
+        nc.vector.memset(sign[:, 1:2], 1.0)
+        warm = const.tile([P, 2], F32)
+        nc.scalar.activation(out=warm[:], in_=sign[:], func=ACT.Sin)
+
+        position_int = const.tile([P, GROUPS_PER_BATCH * SLOTS], I32)
+        nc.gpsimd.iota(
+            position_int[:], pattern=[[GROUP, GROUPS_PER_BATCH], [1, SLOTS]], base=0, channel_multiplier=SLOTS
+        )
+        position = const.tile([P, GROUPS_PER_BATCH * SLOTS], F32)
+        nc.vector.tensor_copy(out=position[:], in_=position_int[:])
+
+        ones = const.tile([P, 8], F32)
+        nc.vector.memset(ones[:], 1.0)
+        coarse = const.tile([P, 8], F32)
+        fine = const.tile([P, 8], F32)
+        for a in range(8):
+            nc.vector.tensor_scalar(
+                out=coarse[:, a : a + 1], in0=ones[:, a : a + 1],
+                scalar1=ROPE_THETA ** (-2.0 * 8 * a / ROPE_DIM) / (2.0 * math.pi), scalar2=None, op0=ALU.mult,
+            )
+            nc.vector.tensor_scalar(
+                out=fine[:, a : a + 1], in0=ones[:, a : a + 1],
+                scalar1=ROPE_THETA ** (-2.0 * a / ROPE_DIM), scalar2=None, op0=ALU.mult,
+            )
+        turns_per_position = const.tile([P, 8, 8], F32)
+        nc.vector.tensor_tensor(
+            out=turns_per_position[:],
+            in0=coarse[:].unsqueeze(2).to_broadcast([P, 8, 8]),
+            in1=fine[:].unsqueeze(1).to_broadcast([P, 8, 8]),
+            op=ALU.mult,
+        )
+
+        def rope_tables(engine, part):
+            rows = slice(part * SLOTS, (part + 1) * SLOTS)
+            shape = [P, SLOTS, ROPE_PAIRS]
+            turns = angle.tile(shape, F32)
+            engine.tensor_tensor(
+                out=turns[:],
+                in0=position[:, rows].unsqueeze(2).to_broadcast(shape),
+                in1=turns_per_position[:].rearrange("p a b -> p (a b)").unsqueeze(1).to_broadcast(shape),
+                op=ALU.mult,
+            )
+            whole = angle.tile(shape, F32)
+            engine.tensor_scalar(
+                out=whole[:], in0=turns[:], scalar1=ROUND_MAGIC, scalar2=ROUND_MAGIC, op0=ALU.add, op1=ALU.subtract
+            )
+            fraction = angle.tile(shape, F32)
+            engine.tensor_tensor(out=fraction[:], in0=turns[:], in1=whole[:], op=ALU.subtract)
+            signed = angle.tile([P, SLOTS * ROPE_PAIRS, 2], F32)
+            engine.tensor_tensor(
+                out=signed[:],
+                in0=fraction[:].rearrange("p n i -> p (n i)").unsqueeze(2).to_broadcast([P, SLOTS * ROPE_PAIRS, 2]),
+                in1=sign[:].unsqueeze(1).to_broadcast([P, SLOTS * ROPE_PAIRS, 2]),
+                op=ALU.mult,
+            )
+            nc.scalar.activation(
+                out=sin_tab[:, rows, :].rearrange("p n d -> p (n d)"),
+                in_=signed[:].rearrange("p m e -> p (m e)"),
+                func=ACT.Sin,
+                scale=2.0 * math.pi,
+            )
+            shifted = angle.tile(shape, F32)
+            engine.tensor_scalar(out=shifted[:], in0=fraction[:], scalar1=0.25, scalar2=None, op0=ALU.add)
+            wrap = angle.tile(shape, F32)
+            engine.tensor_scalar(
+                out=wrap[:], in0=shifted[:], scalar1=ROUND_MAGIC, scalar2=ROUND_MAGIC, op0=ALU.add, op1=ALU.subtract
+            )
+            quarter_on = angle.tile(shape, F32)
+            engine.tensor_tensor(out=quarter_on[:], in0=shifted[:], in1=wrap[:], op=ALU.subtract)
+            nc.scalar.activation(
+                out=cos_tab[:, rows, :].rearrange("p n i -> p (n i)"),
+                in_=quarter_on[:].rearrange("p n i -> p (n i)"),
+                func=ACT.Sin,
+                scale=2.0 * math.pi,
+            )
+
+        rope_tables(nc.vector, 0)
 
         wl_grouped = const.tile([P, PASSES, LATENT, PACK], BF16, align_bytes=64)
         wr_grouped = const.tile([P, PASSES, ROPE_DIM, PACK], BF16, align_bytes=64)
@@ -176,12 +174,15 @@ def tile_mlaattention_pb_t_kernel(tc, hidden_states, Wkva, Wkvb, out_0, out_1):
         wb_codes = const.tile([P, LATENT], U32, align_bytes=64)
         wb_scales = const.tile([P, LATENT], U8, align_bytes=64)
 
-        nc.vector.tensor_copy(out=wl_grouped[:, 0], in_=wa_raw[:, 0, :, 0:LATENT].rearrange("p j n -> p n j"))
-        nc.scalar.copy(out=wl_grouped[:, 1], in_=wa_raw[:, 1, :, 0:LATENT].rearrange("p j n -> p n j"))
-        nc.vector.tensor_copy(out=wr_grouped[:], in_=wa_raw[:, :, :, LATENT:].rearrange("p c j n -> p c n j"))
-        wb_parts = wb_raw[:].rearrange("p j (h two d) -> p two h d j", two=2, d=NOPE_DIM)
-        for part in range(2):
-            nc.vector.tensor_copy(out=wb_grouped[:, part], in_=wb_parts[:, part])
+        for c in range(PASSES):
+            nc.vector.tensor_copy(
+                out=wl_grouped[:, c].rearrange("p (m i) j -> p m j i", i=RUN),
+                in_=wa_raw[:, c, :, 0:LATENT].rearrange("p j (m i) -> p m j i", i=RUN),
+            )
+            nc.scalar.copy(
+                out=wr_grouped[:, c].rearrange("p (m i) j -> p m j i", i=RUN),
+                in_=wa_raw[:, c, :, LATENT:].rearrange("p j (m i) -> p m j i", i=RUN),
+            )
         nc.vector.quantize_mx(
             out=wl_codes[:].rearrange("p c n -> p (c n)").bitcast(FP8X4),
             scales=wl_scales[:].rearrange("p c n -> p (c n)"),
@@ -192,17 +193,21 @@ def tile_mlaattention_pb_t_kernel(tc, hidden_states, Wkva, Wkvb, out_0, out_1):
             scales=wr_scales[:].rearrange("p c n -> p (c n)"),
             in_=wr_grouped[:].rearrange("p c n j -> p (c n j)"),
         )
-        nc.vector.quantize_mx(
-            out=wb_codes[:].bitcast(FP8X4),
-            scales=wb_scales[:],
-            in_=wb_grouped[:].rearrange("p two h d j -> p (two h d j)"),
-        )
+
+        def prepare_wkvb():
+            wb_parts = wb_raw[:].rearrange("p j (h two d) -> p two h d j", two=2, d=NOPE_DIM)
+            for part in range(2):
+                nc.vector.tensor_copy(out=wb_grouped[:, part], in_=wb_parts[:, part])
+            nc.vector.quantize_mx(
+                out=wb_codes[:].bitcast(FP8X4),
+                scales=wb_scales[:],
+                in_=wb_grouped[:].rearrange("p two h d j -> p (two h d j)"),
+            )
 
         live = {}
 
         def slots_of(step):
-            first = (step % STEPS_PER_GROUP) * STEP_SLOTS
-            return step // STEPS_PER_GROUP, first
+            return step // STEPS_PER_GROUP, (step % STEPS_PER_GROUP) * STEP_SLOTS
 
         def transpose_x(step):
             group, first = slots_of(step)
@@ -296,21 +301,16 @@ def tile_mlaattention_pb_t_kernel(tc, hidden_states, Wkva, Wkvb, out_0, out_1):
                 in1=sin_tab[:, table : table + STEP_SLOTS, :].rearrange("p s (i e) -> p s i e", e=2),
                 op=ALU.mult,
             )
+            rope_out = k_out[:, :, first : first + STEP_SLOTS, NOPE_DIM:].rearrange("p h s d -> p s h d")
             nc.vector.tensor_tensor(
-                out=k_out[:, 0, first : first + STEP_SLOTS, NOPE_DIM:],
+                out=rope_out[:, :, 0, :],
                 in0=by_cos[:].rearrange("p s i e -> p s (i e)"),
                 in1=by_sin[:].rearrange("p s i e -> p s (i e)"),
                 op=ALU.add,
             )
-
-        def repeat_for_heads(step):
-            group, first = slots_of(step)
-            k_out, v_out = live["out", group]
-            nc.scalar.copy(
-                out=k_out[:, 1:HEADS, first : first + STEP_SLOTS, NOPE_DIM:],
-                in_=k_out[:, 0:1, first : first + STEP_SLOTS, NOPE_DIM:].to_broadcast(
-                    [P, HEADS - 1, STEP_SLOTS, ROPE_DIM]
-                ),
+            nc.vector.tensor_copy(
+                out=rope_out[:, :, 1:HEADS, :],
+                in_=rope_out[:, :, 0:1, :].to_broadcast([P, STEP_SLOTS, HEADS - 1, ROPE_DIM]),
             )
 
         def expand(step):
@@ -332,6 +332,12 @@ def tile_mlaattention_pb_t_kernel(tc, hidden_states, Wkva, Wkvb, out_0, out_1):
                     )
             live["kv_ps", step] = (nope_ps, v_ps)
 
+        def store(group, first, count):
+            k_out, v_out = live["out", group]
+            slots = slice(first, first + count)
+            nc.sync.dma_start(out=group_rows(out_0, group)[:, :, slots, :], in_=k_out[:, :, slots, :])
+            nc.sync.dma_start(out=group_rows(out_1, group)[:, :, slots, :], in_=v_out[:, :, slots, :])
+
         def finish(step):
             group, first = slots_of(step)
             nope_ps, v_ps = live["kv_ps", step]
@@ -340,28 +346,31 @@ def tile_mlaattention_pb_t_kernel(tc, hidden_states, Wkva, Wkvb, out_0, out_1):
                 out=k_out[:, :, first : first + STEP_SLOTS, 0:NOPE_DIM].rearrange("p h s d -> p s h d"),
                 in_=nope_ps[:].rearrange("p s (h d) -> p s h d", h=HEADS),
             )
-            nc.vector.tensor_copy(
+            nc.scalar.copy(
                 out=v_out[:, :, first : first + STEP_SLOTS, :].rearrange("p h s d -> p s h d"),
                 in_=v_ps[:].rearrange("p s (h d) -> p s h d", h=HEADS),
             )
-            if first + STEP_SLOTS == SLOTS:
-                nc.sync.dma_start(out=k_groups[group], in_=k_out[:].rearrange("p h t d -> p h (t d)"))
-                nc.sync.dma_start(out=v_groups[group], in_=v_out[:].rearrange("p h t d -> p h (t d)"))
+            if group == GROUPS - 1:
+                store(group, first, STEP_SLOTS)
+            elif first + STEP_SLOTS == SLOTS:
+                store(group, 0, SLOTS)
 
         for i in range(STEPS + 3):
             if 0 <= i - 2 < STEPS:
-                rotate(i - 2)
+                quantise_c(i - 2)
+            if 0 <= i - 3 < STEPS:
+                finish(i - 3)
             if i < STEPS:
                 transpose_x(i)
             if 0 <= i - 2 < STEPS:
-                repeat_for_heads(i - 2)
-            if 0 <= i - 3 < STEPS:
-                finish(i - 3)
+                rotate(i - 2)
             if 0 <= i - 1 < STEPS:
                 project(i - 1)
             if i < STEPS:
                 quantise_x(i)
+            if i == 1:
+                prepare_wkvb()
+            if i % STEPS_PER_GROUP == 1 and 0 < (i + 1) // STEPS_PER_GROUP < GROUPS_PER_BATCH:
+                rope_tables(nc.gpsimd, (i + 1) // STEPS_PER_GROUP)
             if 0 <= i - 2 < STEPS:
                 expand(i - 2)
-            if 0 <= i - 1 < STEPS:
-                quantise_c(i - 1)

@@ -34,6 +34,8 @@ STEP_TOKENS = STEP_SLOTS * P
 STEPS_PER_GROUP = SLOTS // STEP_SLOTS
 STEPS = GROUPS * STEPS_PER_GROUP
 
+TAPER_GROUPS = 2
+
 ROUND_MAGIC = 12582912.0
 RUN = 4
 
@@ -43,9 +45,9 @@ FLOPS = 2 * BATCH * SEQ * (D_MODEL * (LATENT + ROPE_DIM) + LATENT * HEADS * (NOP
 def tile_mlaattention_pb_t_kernel(tc, hidden_states, Wkva, Wkvb, out_0, out_1):
     nc = tc.nc
     with ExitStack() as ctx:
+        ctx.enter_context(tc.manual_schedule())
         const = ctx.enter_context(tc.tile_pool(name="const", bufs=1))
         x_pool = ctx.enter_context(tc.tile_pool(name="x_pool", bufs=GROUPS))
-        angle = ctx.enter_context(tc.tile_pool(name="angle", bufs=2))
         stage = ctx.enter_context(tc.tile_pool(name="stage", bufs=3))
         out_pool = ctx.enter_context(tc.tile_pool(name="out_pool", bufs=3))
         psum_xt = ctx.enter_context(tc.psum_pool(name="psum_xt", bufs=2))
@@ -78,6 +80,10 @@ def tile_mlaattention_pb_t_kernel(tc, hidden_states, Wkva, Wkvb, out_0, out_1):
             else:
                 nc.sync.dma_start(out=x_sb[:], in_=x_groups[g])
 
+        position_int = const.tile([P, GROUPS_PER_BATCH * SLOTS], I32)
+        nc.gpsimd.iota(
+            position_int[:], pattern=[[GROUP, GROUPS_PER_BATCH], [1, SLOTS]], base=0, channel_multiplier=SLOTS
+        )
         ident = const.tile([P, P], F32)
         make_identity(nc, ident[:])
 
@@ -89,13 +95,6 @@ def tile_mlaattention_pb_t_kernel(tc, hidden_states, Wkva, Wkvb, out_0, out_1):
         nc.vector.memset(sign[:, 1:2], 1.0)
         warm = const.tile([P, 2], F32)
         nc.scalar.activation(out=warm[:], in_=sign[:], func=ACT.Sin)
-
-        position_int = const.tile([P, GROUPS_PER_BATCH * SLOTS], I32)
-        nc.gpsimd.iota(
-            position_int[:], pattern=[[GROUP, GROUPS_PER_BATCH], [1, SLOTS]], base=0, channel_multiplier=SLOTS
-        )
-        position = const.tile([P, GROUPS_PER_BATCH * SLOTS], F32)
-        nc.vector.tensor_copy(out=position[:], in_=position_int[:])
 
         ones = const.tile([P, 8], F32)
         nc.vector.memset(ones[:], 1.0)
@@ -118,54 +117,75 @@ def tile_mlaattention_pb_t_kernel(tc, hidden_states, Wkva, Wkvb, out_0, out_1):
             op=ALU.mult,
         )
 
-        def rope_tables(engine, part):
-            rows = slice(part * SLOTS, (part + 1) * SLOTS)
-            shape = [P, SLOTS, ROPE_PAIRS]
-            turns = angle.tile(shape, F32)
-            engine.tensor_tensor(
-                out=turns[:],
-                in0=position[:, rows].unsqueeze(2).to_broadcast(shape),
-                in1=turns_per_position[:].rearrange("p a b -> p (a b)").unsqueeze(1).to_broadcast(shape),
+        position = const.tile([P, GROUPS_PER_BATCH * SLOTS], F32)
+        nc.vector.tensor_copy(out=position[:], in_=position_int[:])
+        half_pi = const.tile([P, 1], F32)
+        nc.vector.tensor_scalar(out=half_pi[:], in0=ones[:, 0:1], scalar1=math.pi / 2.0, scalar2=None, op0=ALU.mult)
+
+        wr_grouped = const.tile([P, PASSES, ROPE_DIM, PACK], BF16, align_bytes=64)
+        for c in range(PASSES):
+            nc.scalar.copy(
+                out=wr_grouped[:, c].rearrange("p (m i) j -> p m j i", i=RUN),
+                in_=wa_raw[:, c, :, LATENT:].rearrange("p j (m i) -> p m j i", i=RUN),
+            )
+
+        HALVES = 2
+        half_rows = GROUPS_PER_BATCH * SLOTS // HALVES
+        half_shape = [P, half_rows, ROPE_PAIRS]
+        half_pairs = half_rows * ROPE_PAIRS
+        halves = range(HALVES)
+        turns = [const.tile(half_shape, F32, name="turns%d" % h) for h in halves]
+        whole = [const.tile(half_shape, F32, name="whole%d" % h) for h in halves]
+        fraction = [const.tile(half_shape, F32, name="fraction%d" % h) for h in halves]
+        signed = [const.tile([P, half_pairs, 2], F32, name="signed%d" % h) for h in halves]
+        magnitude = [const.tile(half_shape, F32, name="magnitude%d" % h) for h in halves]
+        for h in halves:
+            nc.vector.tensor_tensor(
+                out=turns[h][:],
+                in0=position[:, h * half_rows : (h + 1) * half_rows].unsqueeze(2).to_broadcast(half_shape),
+                in1=turns_per_position[:].rearrange("p a b -> p (a b)").unsqueeze(1).to_broadcast(half_shape),
                 op=ALU.mult,
             )
-            whole = angle.tile(shape, F32)
-            engine.tensor_scalar(
-                out=whole[:], in0=turns[:], scalar1=ROUND_MAGIC, scalar2=ROUND_MAGIC, op0=ALU.add, op1=ALU.subtract
+        for h in halves:
+            nc.vector.tensor_scalar(
+                out=whole[h][:], in0=turns[h][:],
+                scalar1=ROUND_MAGIC, scalar2=ROUND_MAGIC, op0=ALU.add, op1=ALU.subtract,
             )
-            fraction = angle.tile(shape, F32)
-            engine.tensor_tensor(out=fraction[:], in0=turns[:], in1=whole[:], op=ALU.subtract)
-            signed = angle.tile([P, SLOTS * ROPE_PAIRS, 2], F32)
-            engine.tensor_tensor(
-                out=signed[:],
-                in0=fraction[:].rearrange("p n i -> p (n i)").unsqueeze(2).to_broadcast([P, SLOTS * ROPE_PAIRS, 2]),
-                in1=sign[:].unsqueeze(1).to_broadcast([P, SLOTS * ROPE_PAIRS, 2]),
+        for h in halves:
+            nc.vector.tensor_tensor(out=fraction[h][:], in0=turns[h][:], in1=whole[h][:], op=ALU.subtract)
+        for h in halves:
+            nc.vector.tensor_tensor(
+                out=signed[h][:],
+                in0=fraction[h][:].rearrange("p n i -> p (n i)").unsqueeze(2).to_broadcast([P, half_pairs, 2]),
+                in1=sign[:].unsqueeze(1).to_broadcast([P, half_pairs, 2]),
                 op=ALU.mult,
             )
+        for h in halves:
+            nc.vector.scalar_tensor_tensor(
+                out=magnitude[h][:].rearrange("p n i -> p (n i)"),
+                in0=fraction[h][:].rearrange("p n i -> p (n i)"),
+                scalar=-1.0,
+                in1=fraction[h][:].rearrange("p n i -> p (n i)"),
+                op0=ALU.mult,
+                op1=ALU.max,
+            )
+        for h in halves:
+            rows = slice(h * half_rows, (h + 1) * half_rows)
             nc.scalar.activation(
                 out=sin_tab[:, rows, :].rearrange("p n d -> p (n d)"),
-                in_=signed[:].rearrange("p m e -> p (m e)"),
+                in_=signed[h][:].rearrange("p m e -> p (m e)"),
                 func=ACT.Sin,
                 scale=2.0 * math.pi,
             )
-            shifted = angle.tile(shape, F32)
-            engine.tensor_scalar(out=shifted[:], in0=fraction[:], scalar1=0.25, scalar2=None, op0=ALU.add)
-            wrap = angle.tile(shape, F32)
-            engine.tensor_scalar(
-                out=wrap[:], in0=shifted[:], scalar1=ROUND_MAGIC, scalar2=ROUND_MAGIC, op0=ALU.add, op1=ALU.subtract
-            )
-            quarter_on = angle.tile(shape, F32)
-            engine.tensor_tensor(out=quarter_on[:], in0=shifted[:], in1=wrap[:], op=ALU.subtract)
             nc.scalar.activation(
                 out=cos_tab[:, rows, :].rearrange("p n i -> p (n i)"),
-                in_=quarter_on[:].rearrange("p n i -> p (n i)"),
+                in_=magnitude[h][:].rearrange("p n i -> p (n i)"),
                 func=ACT.Sin,
-                scale=2.0 * math.pi,
+                bias=half_pi[:, 0:1],
+                scale=-2.0 * math.pi,
             )
 
-        rope_tables(nc.vector, 0)
-
         wl_grouped = const.tile([P, PASSES, LATENT, PACK], BF16, align_bytes=64)
-        wr_grouped = const.tile([P, PASSES, ROPE_DIM, PACK], BF16, align_bytes=64)
         wb_grouped = const.tile([P, 2, HEADS, NOPE_DIM, PACK], BF16, align_bytes=64)
         wl_codes = const.tile([P, PASSES, LATENT], U32, align_bytes=64)
         wl_scales = const.tile([P, PASSES, LATENT], U8, align_bytes=64)
@@ -179,15 +199,12 @@ def tile_mlaattention_pb_t_kernel(tc, hidden_states, Wkva, Wkvb, out_0, out_1):
                 out=wl_grouped[:, c].rearrange("p (m i) j -> p m j i", i=RUN),
                 in_=wa_raw[:, c, :, 0:LATENT].rearrange("p j (m i) -> p m j i", i=RUN),
             )
-            nc.scalar.copy(
-                out=wr_grouped[:, c].rearrange("p (m i) j -> p m j i", i=RUN),
-                in_=wa_raw[:, c, :, LATENT:].rearrange("p j (m i) -> p m j i", i=RUN),
+        for c in range(PASSES):
+            nc.vector.quantize_mx(
+                out=wl_codes[:, c, :].bitcast(FP8X4),
+                scales=wl_scales[:, c, :],
+                in_=wl_grouped[:, c].rearrange("p n j -> p (n j)"),
             )
-        nc.vector.quantize_mx(
-            out=wl_codes[:].rearrange("p c n -> p (c n)").bitcast(FP8X4),
-            scales=wl_scales[:].rearrange("p c n -> p (c n)"),
-            in_=wl_grouped[:].rearrange("p c n j -> p (c n j)"),
-        )
         nc.vector.quantize_mx(
             out=wr_codes[:].rearrange("p c n -> p (c n)").bitcast(FP8X4),
             scales=wr_scales[:].rearrange("p c n -> p (c n)"),
@@ -277,7 +294,7 @@ def tile_mlaattention_pb_t_kernel(tc, hidden_states, Wkva, Wkvb, out_0, out_1):
             )
             live["c_codes", step] = (c_codes, c_scales)
 
-        def rotate(step):
+        def rotate_products(step):
             group, first = slots_of(step)
             if first == 0:
                 k_out = out_pool.tile([P, HEADS, SLOTS, NOPE_DIM + ROPE_DIM], F32)
@@ -301,16 +318,26 @@ def tile_mlaattention_pb_t_kernel(tc, hidden_states, Wkva, Wkvb, out_0, out_1):
                 in1=sin_tab[:, table : table + STEP_SLOTS, :].rearrange("p s (i e) -> p s i e", e=2),
                 op=ALU.mult,
             )
-            rope_out = k_out[:, :, first : first + STEP_SLOTS, NOPE_DIM:].rearrange("p h s d -> p s h d")
+            live["products", step] = (by_cos, by_sin)
+
+        def rope_rows(step):
+            group, first = slots_of(step)
+            k_out, v_out = live["out", group]
+            return k_out[:, :, first : first + STEP_SLOTS, NOPE_DIM:].rearrange("p h s d -> p s h d")
+
+        def rotate_sum(step):
+            by_cos, by_sin = live["products", step]
             nc.vector.tensor_tensor(
-                out=rope_out[:, :, 0, :],
+                out=rope_rows(step)[:, :, 0, :],
                 in0=by_cos[:].rearrange("p s i e -> p s (i e)"),
                 in1=by_sin[:].rearrange("p s i e -> p s (i e)"),
                 op=ALU.add,
             )
+
+        def repeat_for_heads(step):
             nc.vector.tensor_copy(
-                out=rope_out[:, :, 1:HEADS, :],
-                in_=rope_out[:, :, 0:1, :].to_broadcast([P, STEP_SLOTS, HEADS - 1, ROPE_DIM]),
+                out=rope_rows(step)[:, :, 1:HEADS, :],
+                in_=rope_rows(step)[:, :, 0:1, :].to_broadcast([P, STEP_SLOTS, HEADS - 1, ROPE_DIM]),
             )
 
         def expand(step):
@@ -338,7 +365,7 @@ def tile_mlaattention_pb_t_kernel(tc, hidden_states, Wkva, Wkvb, out_0, out_1):
             nc.sync.dma_start(out=group_rows(out_0, group)[:, :, slots, :], in_=k_out[:, :, slots, :])
             nc.sync.dma_start(out=group_rows(out_1, group)[:, :, slots, :], in_=v_out[:, :, slots, :])
 
-        def finish(step):
+        def take_k_nope(step):
             group, first = slots_of(step)
             nope_ps, v_ps = live["kv_ps", step]
             k_out, v_out = live["out", group]
@@ -346,31 +373,45 @@ def tile_mlaattention_pb_t_kernel(tc, hidden_states, Wkva, Wkvb, out_0, out_1):
                 out=k_out[:, :, first : first + STEP_SLOTS, 0:NOPE_DIM].rearrange("p h s d -> p s h d"),
                 in_=nope_ps[:].rearrange("p s (h d) -> p s h d", h=HEADS),
             )
+
+        def take_v(step):
+            group, first = slots_of(step)
+            nope_ps, v_ps = live["kv_ps", step]
+            k_out, v_out = live["out", group]
             nc.scalar.copy(
                 out=v_out[:, :, first : first + STEP_SLOTS, :].rearrange("p h s d -> p s h d"),
                 in_=v_ps[:].rearrange("p s (h d) -> p s h d", h=HEADS),
             )
-            if group == GROUPS - 1:
+
+        def store_step(step):
+            group, first = slots_of(step)
+            if group >= GROUPS - TAPER_GROUPS:
                 store(group, first, STEP_SLOTS)
             elif first + STEP_SLOTS == SLOTS:
                 store(group, 0, SLOTS)
 
         for i in range(STEPS + 3):
-            if 0 <= i - 2 < STEPS:
-                quantise_c(i - 2)
-            if 0 <= i - 3 < STEPS:
-                finish(i - 3)
-            if i < STEPS:
-                transpose_x(i)
-            if 0 <= i - 2 < STEPS:
-                rotate(i - 2)
-            if 0 <= i - 1 < STEPS:
-                project(i - 1)
-            if i < STEPS:
-                quantise_x(i)
+            transposing, projecting, expanding, finishing = i, i - 1, i - 2, i - 3
+            if 0 <= expanding < STEPS:
+                rotate_products(expanding)
+                quantise_c(expanding)
+            if 0 <= finishing < STEPS:
+                take_v(finishing)
+            if transposing < STEPS:
+                transpose_x(transposing)
+            if 0 <= finishing < STEPS:
+                take_k_nope(finishing)
+            if 0 <= expanding < STEPS:
+                rotate_sum(expanding)
+            if 0 <= projecting < STEPS:
+                project(projecting)
+            if transposing < STEPS:
+                quantise_x(transposing)
+            if 0 <= expanding < STEPS:
+                repeat_for_heads(expanding)
+            if 0 <= finishing < STEPS:
+                store_step(finishing)
             if i == 1:
                 prepare_wkvb()
-            if i % STEPS_PER_GROUP == 1 and 0 < (i + 1) // STEPS_PER_GROUP < GROUPS_PER_BATCH:
-                rope_tables(nc.gpsimd, (i + 1) // STEPS_PER_GROUP)
-            if 0 <= i - 2 < STEPS:
-                expand(i - 2)
+            if 0 <= expanding < STEPS:
+                expand(expanding)

@@ -34,7 +34,7 @@ STEP_TOKENS = STEP_SLOTS * P
 STEPS_PER_GROUP = SLOTS // STEP_SLOTS
 STEPS = GROUPS * STEPS_PER_GROUP
 
-TAPER_GROUPS = 2
+TAPER_GROUPS = 4
 
 ROUND_MAGIC = 12582912.0
 RUN = 4
@@ -362,8 +362,8 @@ def tile_mlaattention_pb_t_kernel(tc, hidden_states, Wkva, Wkvb, out_0, out_1):
         def store(group, first, count):
             k_out, v_out = live["out", group]
             slots = slice(first, first + count)
-            nc.sync.dma_start(out=group_rows(out_0, group)[:, :, slots, :], in_=k_out[:, :, slots, :])
             nc.sync.dma_start(out=group_rows(out_1, group)[:, :, slots, :], in_=v_out[:, :, slots, :])
+            nc.sync.dma_start(out=group_rows(out_0, group)[:, :, slots, :], in_=k_out[:, :, slots, :])
 
         def take_k_nope(step):
             group, first = slots_of(step)

@@ -88,16 +88,13 @@ def tile_mlaattention_pb_t_kernel(tc, hidden_states, Wkva, Wkvb, out_0, out_1):
         make_identity(nc, ident[:])
 
         cos_tab = const.tile([P, GROUPS_PER_BATCH * SLOTS, ROPE_PAIRS], F32)
-        sin_tab = const.tile([P, GROUPS_PER_BATCH * SLOTS, ROPE_DIM], F32)
-
-        sign = const.tile([P, 2], F32)
-        nc.vector.memset(sign[:, 0:1], -1.0)
-        nc.vector.memset(sign[:, 1:2], 1.0)
-        warm = const.tile([P, 2], F32)
-        nc.scalar.activation(out=warm[:], in_=sign[:], func=ACT.Sin)
+        sin_tab = const.tile([P, GROUPS_PER_BATCH * SLOTS, 2, ROPE_PAIRS], F32)
 
         ones = const.tile([P, 8], F32)
         nc.vector.memset(ones[:], 1.0)
+        warm = const.tile([P, 8], F32)
+        nc.scalar.activation(out=warm[:], in_=ones[:], func=ACT.Sin)
+
         coarse = const.tile([P, 8], F32)
         fine = const.tile([P, 8], F32)
         for a in range(8):
@@ -122,22 +119,13 @@ def tile_mlaattention_pb_t_kernel(tc, hidden_states, Wkva, Wkvb, out_0, out_1):
         half_pi = const.tile([P, 1], F32)
         nc.vector.tensor_scalar(out=half_pi[:], in0=ones[:, 0:1], scalar1=math.pi / 2.0, scalar2=None, op0=ALU.mult)
 
-        wr_grouped = const.tile([P, PASSES, ROPE_DIM, PACK], BF16, align_bytes=64)
-        for c in range(PASSES):
-            nc.scalar.copy(
-                out=wr_grouped[:, c].rearrange("p (m i) j -> p m j i", i=RUN),
-                in_=wa_raw[:, c, :, LATENT:].rearrange("p j (m i) -> p m j i", i=RUN),
-            )
-
         HALVES = 2
         half_rows = GROUPS_PER_BATCH * SLOTS // HALVES
         half_shape = [P, half_rows, ROPE_PAIRS]
-        half_pairs = half_rows * ROPE_PAIRS
         halves = range(HALVES)
         turns = [const.tile(half_shape, F32, name="turns%d" % h) for h in halves]
         whole = [const.tile(half_shape, F32, name="whole%d" % h) for h in halves]
         fraction = [const.tile(half_shape, F32, name="fraction%d" % h) for h in halves]
-        signed = [const.tile([P, half_pairs, 2], F32, name="signed%d" % h) for h in halves]
         magnitude = [const.tile(half_shape, F32, name="magnitude%d" % h) for h in halves]
         for h in halves:
             nc.vector.tensor_tensor(
@@ -153,37 +141,29 @@ def tile_mlaattention_pb_t_kernel(tc, hidden_states, Wkva, Wkvb, out_0, out_1):
             )
         for h in halves:
             nc.vector.tensor_tensor(out=fraction[h][:], in0=turns[h][:], in1=whole[h][:], op=ALU.subtract)
+
         for h in halves:
-            nc.vector.tensor_tensor(
-                out=signed[h][:],
-                in0=fraction[h][:].rearrange("p n i -> p (n i)").unsqueeze(2).to_broadcast([P, half_pairs, 2]),
-                in1=sign[:].unsqueeze(1).to_broadcast([P, half_pairs, 2]),
-                op=ALU.mult,
+            nc.scalar.activation(out=magnitude[h][:], in_=fraction[h][:], func=ACT.Abs)
+        wr_grouped = const.tile([P, PASSES, ROPE_DIM, PACK], BF16, align_bytes=64)
+        for c in range(PASSES):
+            nc.scalar.copy(
+                out=wr_grouped[:, c].rearrange("p (m i) j -> p m j i", i=RUN),
+                in_=wa_raw[:, c, :, LATENT:].rearrange("p j (m i) -> p m j i", i=RUN),
             )
-        for h in halves:
-            nc.vector.scalar_tensor_tensor(
-                out=magnitude[h][:].rearrange("p n i -> p (n i)"),
-                in0=fraction[h][:].rearrange("p n i -> p (n i)"),
-                scalar=-1.0,
-                in1=fraction[h][:].rearrange("p n i -> p (n i)"),
-                op0=ALU.mult,
-                op1=ALU.max,
-            )
-        for h in halves:
+
+        def sine_pass(number):
+            h, kind = divmod(number, 3)
             rows = slice(h * half_rows, (h + 1) * half_rows)
-            nc.scalar.activation(
-                out=sin_tab[:, rows, :].rearrange("p n d -> p (n d)"),
-                in_=signed[h][:].rearrange("p m e -> p (m e)"),
-                func=ACT.Sin,
-                scale=2.0 * math.pi,
-            )
-            nc.scalar.activation(
-                out=cos_tab[:, rows, :].rearrange("p n i -> p (n i)"),
-                in_=magnitude[h][:].rearrange("p n i -> p (n i)"),
-                func=ACT.Sin,
-                bias=half_pi[:, 0:1],
-                scale=-2.0 * math.pi,
-            )
+            if kind == 0:
+                nc.scalar.activation(
+                    out=cos_tab[:, rows, :], in_=magnitude[h][:], func=ACT.Sin,
+                    bias=half_pi[:, 0:1], scale=-2.0 * math.pi,
+                )
+            else:
+                sign = (-1.0, 1.0)[kind - 1]
+                nc.scalar.activation(
+                    out=sin_tab[:, rows, kind - 1, :], in_=fraction[h][:], func=ACT.Sin, scale=sign * 2.0 * math.pi
+                )
 
         wl_grouped = const.tile([P, PASSES, LATENT, PACK], BF16, align_bytes=64)
         wb_grouped = const.tile([P, 2, HEADS, NOPE_DIM, PACK], BF16, align_bytes=64)
@@ -315,7 +295,7 @@ def tile_mlaattention_pb_t_kernel(tc, hidden_states, Wkva, Wkvb, out_0, out_1):
             nc.vector.tensor_tensor(
                 out=by_sin[:],
                 in0=rope_pairs[:, :, :, ::-1],
-                in1=sin_tab[:, table : table + STEP_SLOTS, :].rearrange("p s (i e) -> p s i e", e=2),
+                in1=sin_tab[:, table : table + STEP_SLOTS, :, :].rearrange("p s e i -> p s i e"),
                 op=ALU.mult,
             )
             live["products", step] = (by_cos, by_sin)
@@ -399,6 +379,8 @@ def tile_mlaattention_pb_t_kernel(tc, hidden_states, Wkva, Wkvb, out_0, out_1):
                 take_v(finishing)
             if transposing < STEPS:
                 transpose_x(transposing)
+            for number in range(2 * i, min(2 * i + 2, 3 * HALVES)):
+                sine_pass(number)
             if 0 <= finishing < STEPS:
                 take_k_nope(finishing)
             if 0 <= expanding < STEPS:

import math
from contextlib import ExitStack

import concourse.mybir as mybir
from concourse.masks import make_identity

F32 = mybir.dt.float32
BF16 = mybir.dt.bfloat16
I32 = mybir.dt.int32
U32 = mybir.dt.uint32
U8 = mybir.dt.uint8
FP8X4 = mybir.dt.float8_e4m3fn_x4
ALU = mybir.AluOpType
ACT = mybir.ActivationFunctionType

P = 128
PACK = 4

BATCH, SEQ, D_MODEL = 2, 2048, 1024
HEADS, LATENT, ROPE_DIM, NOPE_DIM, V_DIM = 4, 512, 128, 64, 64
ROPE_THETA = 10000.0
ROPE_PAIRS = ROPE_DIM // 2

PASSES = D_MODEL // (P * PACK)
LATENT_TILES = LATENT // P

SLOTS = 4
GROUP = P * SLOTS
GROUPS = BATCH * SEQ // GROUP
GROUPS_PER_BATCH = SEQ // GROUP

STEP_SLOTS = 2
STEP_TOKENS = STEP_SLOTS * P
STEPS_PER_GROUP = SLOTS // STEP_SLOTS
STEPS = GROUPS * STEPS_PER_GROUP

TAPER_GROUPS = 4

ROUND_MAGIC = 12582912.0
RUN = 4

FLOPS = 2 * BATCH * SEQ * (D_MODEL * (LATENT + ROPE_DIM) + LATENT * HEADS * (NOPE_DIM + V_DIM))


def tile_mlaattention_pb_t_kernel(tc, hidden_states, Wkva, Wkvb, out_0, out_1):
    nc = tc.nc
    with ExitStack() as ctx:
        ctx.enter_context(tc.manual_schedule())
        const = ctx.enter_context(tc.tile_pool(name="const", bufs=1))
        x_pool = ctx.enter_context(tc.tile_pool(name="x_pool", bufs=GROUPS))
        stage = ctx.enter_context(tc.tile_pool(name="stage", bufs=3))
        out_pool = ctx.enter_context(tc.tile_pool(name="out_pool", bufs=3))
        psum_xt = ctx.enter_context(tc.psum_pool(name="psum_xt", bufs=2))
        psum_c = ctx.enter_context(tc.psum_pool(name="psum_c", bufs=2))
        psum_rope = ctx.enter_context(tc.psum_pool(name="psum_rope", bufs=1))
        psum_kv = ctx.enter_context(tc.psum_pool(name="psum_kv", bufs=3))

        x_groups = hidden_states.flatten_outer_dims().rearrange("(g p t) d -> g p t d", p=P, t=SLOTS)

        def group_rows(out, group):
            batch, part = divmod(group, GROUPS_PER_BATCH)
            rows = out[batch, :, part * GROUP : (part + 1) * GROUP, :]
            return rows.rearrange("h (p t) d -> p h t d", t=SLOTS)

        wa_raw = const.tile([P, PASSES, PACK, LATENT + ROPE_DIM], BF16)
        wa_rows = Wkva.rearrange("(c u q e) n -> c q u (e n)", c=PASSES, u=2, e=2)
        for c in range(PASSES):
            nc.sync.dma_start(out=wa_raw[:, c].rearrange("q (u e) n -> q u (e n)", e=2), in_=wa_rows[c])
        wb_raw = const.tile([P, PACK, LATENT], BF16)
        x_tiles = []
        for g in range(GROUPS):
            x_sb = x_pool.tile([P, SLOTS, D_MODEL], BF16)
            x_tiles.append(x_sb)
            if g == 0:
                for first in range(0, SLOTS, STEP_SLOTS):
                    nc.sync.dma_start(
                        out=x_sb[:, first : first + STEP_SLOTS, :], in_=x_groups[g][:, first : first + STEP_SLOTS, :]
                    )
                nc.sync.dma_start(out=wb_raw[:], in_=Wkvb.rearrange("(j q) n -> q j n", q=P))
            else:
                nc.sync.dma_start(out=x_sb[:], in_=x_groups[g])

        position_int = const.tile([P, GROUPS_PER_BATCH * SLOTS], I32)
        nc.gpsimd.iota(
            position_int[:], pattern=[[GROUP, GROUPS_PER_BATCH], [1, SLOTS]], base=0, channel_multiplier=SLOTS
        )
        ident = const.tile([P, P], F32)
        make_identity(nc, ident[:])

        cos_tab = const.tile([P, GROUPS_PER_BATCH * SLOTS, ROPE_PAIRS], F32)
        sin_tab = const.tile([P, GROUPS_PER_BATCH * SLOTS, 2, ROPE_PAIRS], F32)

        ones = const.tile([P, 8], F32)
        nc.vector.memset(ones[:], 1.0)
        warm = const.tile([P, 8], F32)
        nc.scalar.activation(out=warm[:], in_=ones[:], func=ACT.Sin)

        coarse = const.tile([P, 8], F32)
        fine = const.tile([P, 8], F32)
        for a in range(8):
            nc.vector.tensor_scalar(
                out=coarse[:, a : a + 1], in0=ones[:, a : a + 1],
                scalar1=ROPE_THETA ** (-2.0 * 8 * a / ROPE_DIM) / (2.0 * math.pi), scalar2=None, op0=ALU.mult,
            )
            nc.vector.tensor_scalar(
                out=fine[:, a : a + 1], in0=ones[:, a : a + 1],
                scalar1=ROPE_THETA ** (-2.0 * a / ROPE_DIM), scalar2=None, op0=ALU.mult,
            )
        turns_per_position = const.tile([P, 8, 8], F32)
        nc.vector.tensor_tensor(
            out=turns_per_position[:],
            in0=coarse[:].unsqueeze(2).to_broadcast([P, 8, 8]),
            in1=fine[:].unsqueeze(1).to_broadcast([P, 8, 8]),
            op=ALU.mult,
        )

        position = const.tile([P, GROUPS_PER_BATCH * SLOTS], F32)
        nc.vector.tensor_copy(out=position[:], in_=position_int[:])
        half_pi = const.tile([P, 1], F32)
        nc.vector.tensor_scalar(out=half_pi[:], in0=ones[:, 0:1], scalar1=math.pi / 2.0, scalar2=None, op0=ALU.mult)

        HALVES = 2
        half_rows = GROUPS_PER_BATCH * SLOTS // HALVES
        half_shape = [P, half_rows, ROPE_PAIRS]
        halves = range(HALVES)
        turns = [const.tile(half_shape, F32, name="turns%d" % h) for h in halves]
        whole = [const.tile(half_shape, F32, name="whole%d" % h) for h in halves]
        fraction = [const.tile(half_shape, F32, name="fraction%d" % h) for h in halves]
        magnitude = [const.tile(half_shape, F32, name="magnitude%d" % h) for h in halves]
        for h in halves:
            nc.vector.tensor_tensor(
                out=turns[h][:],
                in0=position[:, h * half_rows : (h + 1) * half_rows].unsqueeze(2).to_broadcast(half_shape),
                in1=turns_per_position[:].rearrange("p a b -> p (a b)").unsqueeze(1).to_broadcast(half_shape),
                op=ALU.mult,
            )
        for h in halves:
            nc.vector.tensor_scalar(
                out=whole[h][:], in0=turns[h][:],
                scalar1=ROUND_MAGIC, scalar2=ROUND_MAGIC, op0=ALU.add, op1=ALU.subtract,
            )
        for h in halves:
            nc.vector.tensor_tensor(out=fraction[h][:], in0=turns[h][:], in1=whole[h][:], op=ALU.subtract)

        for h in halves:
            nc.scalar.activation(out=magnitude[h][:], in_=fraction[h][:], func=ACT.Abs)
        wr_grouped = const.tile([P, PASSES, ROPE_DIM, PACK], BF16, align_bytes=64)
        for c in range(PASSES):
            nc.scalar.copy(
                out=wr_grouped[:, c].rearrange("p (m i) j -> p m j i", i=RUN),
                in_=wa_raw[:, c, :, LATENT:].rearrange("p j (m i) -> p m j i", i=RUN),
            )

        def sine_pass(number):
            h, kind = divmod(number, 3)
            rows = slice(h * half_rows, (h + 1) * half_rows)
            if kind == 0:
                nc.scalar.activation(
                    out=cos_tab[:, rows, :], in_=magnitude[h][:], func=ACT.Sin,
                    bias=half_pi[:, 0:1], scale=-2.0 * math.pi,
                )
            else:
                sign = (-1.0, 1.0)[kind - 1]
                nc.scalar.activation(
                    out=sin_tab[:, rows, kind - 1, :], in_=fraction[h][:], func=ACT.Sin, scale=sign * 2.0 * math.pi
                )

        wl_grouped = const.tile([P, PASSES, LATENT, PACK], BF16, align_bytes=64)
        wb_grouped = const.tile([P, 2, HEADS, NOPE_DIM, PACK], BF16, align_bytes=64)
        wl_codes = const.tile([P, PASSES, LATENT], U32, align_bytes=64)
        wl_scales = const.tile([P, PASSES, LATENT], U8, align_bytes=64)
        wr_codes = const.tile([P, PASSES, ROPE_DIM], U32, align_bytes=64)
        wr_scales = const.tile([P, PASSES, ROPE_DIM], U8, align_bytes=64)
        wb_codes = const.tile([P, LATENT], U32, align_bytes=64)
        wb_scales = const.tile([P, LATENT], U8, align_bytes=64)

        for c in range(PASSES):
            nc.vector.tensor_copy(
                out=wl_grouped[:, c].rearrange("p (m i) j -> p m j i", i=RUN),
                in_=wa_raw[:, c, :, 0:LATENT].rearrange("p j (m i) -> p m j i", i=RUN),
            )
        for c in range(PASSES):
            nc.vector.quantize_mx(
                out=wl_codes[:, c, :].bitcast(FP8X4),
                scales=wl_scales[:, c, :],
                in_=wl_grouped[:, c].rearrange("p n j -> p (n j)"),
            )
        nc.vector.quantize_mx(
            out=wr_codes[:].rearrange("p c n -> p (c n)").bitcast(FP8X4),
            scales=wr_scales[:].rearrange("p c n -> p (c n)"),
            in_=wr_grouped[:].rearrange("p c n j -> p (c n j)"),
        )

        def prepare_wkvb():
            wb_parts = wb_raw[:].rearrange("p j (h two d) -> p two h d j", two=2, d=NOPE_DIM)
            for part in range(2):
                nc.vector.tensor_copy(out=wb_grouped[:, part], in_=wb_parts[:, part])
            nc.vector.quantize_mx(
                out=wb_codes[:].bitcast(FP8X4),
                scales=wb_scales[:],
                in_=wb_grouped[:].rearrange("p two h d j -> p (two h d j)"),
            )

        live = {}

        def slots_of(step):
            return step // STEPS_PER_GROUP, (step % STEPS_PER_GROUP) * STEP_SLOTS

        def transpose_x(step):
            group, first = slots_of(step)
            x_grouped = stage.tile([P, PASSES, STEP_TOKENS, 2], F32, align_bytes=64)
            for s in range(STEP_SLOTS):
                x_words = x_tiles[group][:, first + s, :].bitcast(F32)
                xt = psum_xt.tile([P, PASSES * 2, P], F32)
                for block in range(PASSES * 2):
                    nc.tensor.transpose(xt[:, block, :], x_words[:, block * P : (block + 1) * P], ident[:])
                nc.scalar.copy(
                    out=x_grouped[:, :, s * P : (s + 1) * P, :],
                    in_=xt[:].rearrange("q (c u) r -> q c r u", u=2),
                )
            live["x_grouped", step] = x_grouped

        def quantise_x(step):
            x_codes = stage.tile([P, PASSES, STEP_TOKENS], U32, align_bytes=64)
            x_scales = stage.tile([P, PASSES, STEP_TOKENS], U8, align_bytes=64)
            nc.vector.quantize_mx(
                out=x_codes[:].rearrange("p c r -> p (c r)").bitcast(FP8X4),
                scales=x_scales[:].rearrange("p c r -> p (c r)"),
                in_=live["x_grouped", step][:].rearrange("p c r u -> p (c r u)").bitcast(BF16),
            )
            live["x_codes", step] = (x_codes, x_scales)

        def project(step):
            x_codes, x_scales = live["x_codes", step]
            c_grouped = stage.tile([P, STEP_TOKENS, PACK], BF16, align_bytes=64)
            for s in range(STEP_SLOTS):
                tokens = slice(s * P, (s + 1) * P)
                c_ps = psum_c.tile([P, LATENT_TILES, P], F32)
                for j in range(LATENT_TILES):
                    for c in range(PASSES):
                        nc.tensor.matmul_mx(
                            out=c_ps[:, j, :],
                            lhsT=wl_codes[:, c, j * P : (j + 1) * P].bitcast(FP8X4),
                            lhsT_scale=wl_scales[:, c, j * P : (j + 1) * P],
                            rhs=x_codes[:, c, tokens].bitcast(FP8X4),
                            rhs_scale=x_scales[:, c, tokens],
                            start=(c == 0),
                            stop=(c == PASSES - 1),
                        )
                nc.scalar.copy(out=c_grouped[:, tokens, :], in_=c_ps[:].rearrange("q j r -> q r j"))
            rope_ps = psum_rope.tile([P, STEP_SLOTS, ROPE_DIM], F32)
            for s in range(STEP_SLOTS):
                tokens = slice(s * P, (s + 1) * P)
                for c in range(PASSES):
                    nc.tensor.matmul_mx(
                        out=rope_ps[:, s, :],
                        lhsT=x_codes[:, c, tokens].bitcast(FP8X4),
                        lhsT_scale=x_scales[:, c, tokens],
                        rhs=wr_codes[:, c, :].bitcast(FP8X4),
                        rhs_scale=wr_scales[:, c, :],
                        start=(c == 0),
                        stop=(c == PASSES - 1),
                    )
            live["c_grouped", step] = c_grouped
            live["rope_ps", step] = rope_ps

        def quantise_c(step):
            c_codes = stage.tile([P, STEP_TOKENS], U32, align_bytes=64)
            c_scales = stage.tile([P, STEP_TOKENS], U8, align_bytes=64)
            nc.vector.quantize_mx(
                out=c_codes[:].bitcast(FP8X4),
                scales=c_scales[:],
                in_=live["c_grouped", step][:].rearrange("p r j -> p (r j)"),
            )
            live["c_codes", step] = (c_codes, c_scales)

        def rotate_products(step):
            group, first = slots_of(step)
            if first == 0:
                k_out = out_pool.tile([P, HEADS, SLOTS, NOPE_DIM + ROPE_DIM], F32)
                v_out = out_pool.tile([P, HEADS, SLOTS, V_DIM], F32)
                live["out", group] = (k_out, v_out)
            k_out, v_out = live["out", group]
            table = (group % GROUPS_PER_BATCH) * SLOTS + first
            pair_shape = [P, STEP_SLOTS, ROPE_PAIRS, 2]
            rope_pairs = live["rope_ps", step][:].rearrange("p s (i e) -> p s i e", e=2)
            by_cos = stage.tile(pair_shape, F32)
            by_sin = stage.tile(pair_shape, F32)
            nc.vector.tensor_tensor(
                out=by_cos[:],
                in0=rope_pairs,
                in1=cos_tab[:, table : table + STEP_SLOTS, :].unsqueeze(3).to_broadcast(pair_shape),
                op=ALU.mult,
            )
            nc.vector.tensor_tensor(
                out=by_sin[:],
                in0=rope_pairs[:, :, :, ::-1],
                in1=sin_tab[:, table : table + STEP_SLOTS, :, :].rearrange("p s e i -> p s i e"),
                op=ALU.mult,
            )
            live["products", step] = (by_cos, by_sin)

        def rope_rows(step):
            group, first = slots_of(step)
            k_out, v_out = live["out", group]
            return k_out[:, :, first : first + STEP_SLOTS, NOPE_DIM:].rearrange("p h s d -> p s h d")

        def rotate_sum(step):
            by_cos, by_sin = live["products", step]
            nc.vector.tensor_tensor(
                out=rope_rows(step)[:, :, 0, :],
                in0=by_cos[:].rearrange("p s i e -> p s (i e)"),
                in1=by_sin[:].rearrange("p s i e -> p s (i e)"),
                op=ALU.add,
            )

        def repeat_for_heads(step):
            nc.vector.tensor_copy(
                out=rope_rows(step)[:, :, 1:HEADS, :],
                in_=rope_rows(step)[:, :, 0:1, :].to_broadcast([P, STEP_SLOTS, HEADS - 1, ROPE_DIM]),
            )

        def expand(step):
            c_codes, c_scales = live["c_codes", step]
            nope_ps = psum_kv.tile([P, STEP_SLOTS, HEADS * NOPE_DIM], F32, tag="kv")
            v_ps = psum_kv.tile([P, STEP_SLOTS, HEADS * V_DIM], F32, tag="kv")
            half = HEADS * NOPE_DIM
            for s in range(STEP_SLOTS):
                tokens = slice(s * P, (s + 1) * P)
                for part, bank in enumerate((nope_ps, v_ps)):
                    nc.tensor.matmul_mx(
                        out=bank[:, s, :],
                        lhsT=c_codes[:, tokens].bitcast(FP8X4),
                        lhsT_scale=c_scales[:, tokens],
                        rhs=wb_codes[:, part * half : (part + 1) * half].bitcast(FP8X4),
                        rhs_scale=wb_scales[:, part * half : (part + 1) * half],
                        start=True,
                        stop=True,
                    )
            live["kv_ps", step] = (nope_ps, v_ps)

        def store(group, first, count):
            k_out, v_out = live["out", group]
            slots = slice(first, first + count)
            nc.sync.dma_start(out=group_rows(out_1, group)[:, :, slots, :], in_=v_out[:, :, slots, :])
            nc.sync.dma_start(out=group_rows(out_0, group)[:, :, slots, :], in_=k_out[:, :, slots, :])

        def take_k_nope(step):
            group, first = slots_of(step)
            nope_ps, v_ps = live["kv_ps", step]
            k_out, v_out = live["out", group]
            nc.vector.tensor_copy(
                out=k_out[:, :, first : first + STEP_SLOTS, 0:NOPE_DIM].rearrange("p h s d -> p s h d"),
                in_=nope_ps[:].rearrange("p s (h d) -> p s h d", h=HEADS),
            )

        def take_v(step):
            group, first = slots_of(step)
            nope_ps, v_ps = live["kv_ps", step]
            k_out, v_out = live["out", group]
            nc.scalar.copy(
                out=v_out[:, :, first : first + STEP_SLOTS, :].rearrange("p h s d -> p s h d"),
                in_=v_ps[:].rearrange("p s (h d) -> p s h d", h=HEADS),
            )

        def store_step(step):
            group, first = slots_of(step)
            if group >= GROUPS - TAPER_GROUPS:
                store(group, first, STEP_SLOTS)
            elif first + STEP_SLOTS == SLOTS:
                store(group, 0, SLOTS)

        for i in range(STEPS + 3):
            transposing, projecting, expanding, finishing = i, i - 1, i - 2, i - 3
            if 0 <= expanding < STEPS:
                rotate_products(expanding)
                quantise_c(expanding)
            if 0 <= finishing < STEPS:
                take_v(finishing)
            if transposing < STEPS:
                transpose_x(transposing)
            for number in range(2 * i, min(2 * i + 2, 3 * HALVES)):
                sine_pass(number)
            if 0 <= finishing < STEPS:
                take_k_nope(finishing)
            if 0 <= expanding < STEPS:
                rotate_sum(expanding)
            if 0 <= projecting < STEPS:
                project(projecting)
            if transposing < STEPS:
                quantise_x(transposing)
            if 0 <= expanding < STEPS:
                repeat_for_heads(expanding)
            if 0 <= finishing < STEPS:
                store_step(finishing)
            if i == 1:
                prepare_wkvb()
            if 0 <= expanding < STEPS:
                expand(expanding)
